import numpy as np
import ml_dtypes


def mxq(x, axis, fmt="e4m3"):
    dtype, down = {"e4m3": (ml_dtypes.float8_e4m3fn, 7), "e5m2": (ml_dtypes.float8_e5m2, 14)}[fmt]
    v = np.moveaxis(np.asarray(x, np.float32).astype(ml_dtypes.bfloat16).astype(np.float64), axis, -1)
    blocks = v.reshape(v.shape[:-1] + (-1, 32))
    amax = np.abs(blocks).max(-1, keepdims=True)
    byte = np.maximum(np.where(amax > 0, np.frexp(amax)[1] - 1 + 127, 0) - down, 1)
    scale = np.exp2(byte - 127.0)
    codes = (blocks / scale).astype(np.float32).astype(dtype).astype(np.float64)
    return np.moveaxis((codes * scale).reshape(v.shape), -1, axis)


WIDE = False


def mx_kscale(k):
    if not WIDE:
        return np.ones(k)
    levels = np.array([10, -10, 5, -5, 0])
    a = np.random.permutation(np.resize(levels, k // 512 * 4)).reshape(k // 512, 4)
    idx = np.arange(k)
    return np.exp2(a[idx // 512, idx % 128 // 32])


BF16 = ml_dtypes.bfloat16


def bf(x):
    return np.asarray(x, np.float32).astype(BF16)


def f64(x):
    return np.asarray(x).astype(np.float64)


B, C, H, W, O, HS, WS, K = 2, 512, 64, 64, 128, 4, 4, 3
PAD = 0
NI, NJ = H // HS, W // WS


def setup_inputs():
    s = mx_kscale(C)
    fan_in = C * K * K
    return {"x": bf(np.random.standard_normal((B, C, H, W)) * s[None, :, None, None]),
            "weight": bf(np.random.standard_normal((HS, WS, O, C, K, K)) / np.sqrt(fan_in) / s[None, None, None, :, None, None]),
            "bias": bf(np.random.standard_normal((HS, WS, O)) * 0.5)}


def reference(x, weight, bias):
    x, weight = f64(x), f64(weight)
    xs = x.reshape(B, C, NI, HS, NJ, WS).transpose(3, 5, 0, 2, 4, 1).reshape(HS, WS, B * NI * NJ, C)
    ws = np.stack([np.roll(weight[:, :, :, :, u, v], (u, v), (0, 1)) for u in range(K) for v in range(K)], axis=2)
    ws = ws.transpose(0, 1, 4, 2, 3).reshape(HS, WS, C, K * K * O)
    z = mxq(xs, 3, "e4m3") @ mxq(ws, 2, "e4m3")
    zi = z.reshape(HS, WS, B, NI, NJ, K, K, O).transpose(2, 3, 0, 4, 1, 5, 6, 7).reshape(B, H, W, K, K, O)
    zp = np.pad(zi, ((0, 0), (0, WS - 2 + PAD), (0, HS - 2 + PAD), (0, 0), (0, 0), (0, 0)))
    out = sum(zp[:, u:u + H, v:v + W, u, v, :] for u in range(K) for v in range(K))
    out = out.transpose(0, 3, 1, 2).reshape(B, O, NI, HS, NJ, WS)
    out = out + f64(bias).transpose(2, 0, 1)[None, :, None, :, None, :]
    return out.reshape(B, O, H, W)

@@ -1,0 +1,224 @@
+from contextlib import ExitStack
+
+import concourse.mybir as mybir
+from concourse.masks import make_identity
+
+F32 = mybir.dt.float32
+BF16 = mybir.dt.bfloat16
+U8 = mybir.dt.uint8
+U32 = mybir.dt.uint32
+I32 = mybir.dt.int32
+FP8X4 = mybir.dt.float8_e4m3fn_x4
+ADD = mybir.AluOpType.add
+MULT = mybir.AluOpType.mult
+IDENT = mybir.ActivationFunctionType.Identity
+
+P = 128
+B, C, H, W, O = 2, 512, 64, 64, 128
+HS, WS, K = 4, 4, 3
+NI, NJ = H // HS, W // WS
+TAPS = K * K
+NCLS = HS * WS
+PIX = NI * NJ
+PADPIX = PIX + NJ
+XROWS = 16
+XI = XROWS // HS
+NCHUNK = H // XROWS
+FLOPS = 2 * B * O * H * W * C * TAPS
+
+X_SCALAR_PH = (2, 3)
+W_SCALAR_UNITS = (7, 8)
+
+
+def tile_patternconv_t_kernel(tc, x, weight, bias, out):
+    nc = tc.nc
+    with ExitStack() as ctx:
+        const = ctx.enter_context(tc.tile_pool(name="const", bufs=1))
+        raw = ctx.enter_context(tc.tile_pool(name="raw", bufs=6))
+        st2 = ctx.enter_context(tc.tile_pool(name="st2", bufs=3))
+        grp = ctx.enter_context(tc.tile_pool(name="grp", bufs=2))
+        wq = ctx.enter_context(tc.tile_pool(name="wq", bufs=3))
+        res = ctx.enter_context(tc.tile_pool(name="res", bufs=2))
+        psum = ctx.enter_context(tc.psum_pool(name="psum", bufs=2))
+
+        ident_f = const.tile([P, P], F32)
+        make_identity(nc, ident_f[:])
+        ident_b = const.tile([P, P], BF16)
+        make_identity(nc, ident_b[:])
+
+        xc = const.tile([P, NCLS * B * PADPIX], U32, align_bytes=64)
+        xs = const.tile([P, NCLS * B * PIX], U8, align_bytes=64)
+        xs1 = const.tile([P, 2 * WS * B * PIX], U8, align_bytes=64)
+        xc4 = xc[:].rearrange("p (k b c) -> p k b c", k=NCLS, b=B)
+        xs4 = xs[:].rearrange("p (k b c) -> p k b c", k=NCLS, b=B)
+        xs14 = xs1[:].rearrange("p (k b c) -> p k b c", k=2 * WS, b=B)
+        nc.vector.memset(xs[:].bitcast(I32), 0)
+        nc.vector.memset(xs1[:].bitcast(I32), 0)
+        nc.vector.memset(
+            xc[:].bitcast(I32).rearrange("p (g c) -> p g c", c=PADPIX)[:, :, PIX:PADPIX], 0
+        )
+
+        bias_rows = const.tile([P, P], BF16)
+        nc.vector.memset(bias_rows[:], 0.0)
+        nc.sync.dma_start(out=bias_rows[0:NCLS, :], in_=bias.rearrange("h w o -> (h w) o"))
+        bias_ps = psum.tile([P, P], BF16, tag="pt", bufs=4)
+        nc.tensor.transpose(bias_ps[:], bias_rows[:], ident_b[:])
+        bias_sb = const.tile([P, NCLS], F32)
+        nc.vector.tensor_copy(out=bias_sb[:], in_=bias_ps[:, 0:NCLS])
+
+        for b in range(B):
+            for ch in range(NCHUNK):
+                xr = raw.tile([P, 4, XROWS * W], BF16, tag="raw")
+                nc.sync.dma_start(
+                    out=xr[:],
+                    in_=x[b, :, ch * XROWS : (ch + 1) * XROWS, :].rearrange(
+                        "(p t) y z -> p t (y z)", t=4
+                    ),
+                )
+                xg = st2.tile([P, NCLS, XI * NJ * 4], BF16, tag="st2", align_bytes=64)
+                src = xr[:].rearrange(
+                    "p t (i a j q) -> p a q i j t", i=XI, a=HS, j=NJ, q=WS
+                )
+                dst = xg[:].rearrange(
+                    "p (a q) (i j t) -> p a q i j t", a=HS, q=WS, i=XI, j=NJ, t=4
+                )
+                for ph in range(HS):
+                    if ph in X_SCALAR_PH:
+                        for q in range(WS):
+                            nc.scalar.copy(out=dst[:, ph, q], in_=src[:, ph, q])
+                    else:
+                        nc.vector.tensor_copy(out=dst[:, ph], in_=src[:, ph])
+                cols = slice(ch * XI * NJ, (ch + 1) * XI * NJ)
+                for cls in range(NCLS):
+                    nc.vector.quantize_mx(
+                        out=xc4[:, cls, b, cols].bitcast(FP8X4),
+                        scales=xs4[:, cls, b, cols],
+                        in_=xg[:, cls, :],
+                    )
+            s_src = xs[:].bitcast(I32).rearrange("p (k b c) -> p k b c", k=NCLS, b=B)
+            s_dst = xs1[:].bitcast(I32).rearrange("p (k b c) -> p k b c", k=2 * WS, b=B)
+            nw = PIX // 4
+            sh = NJ // 4
+            nc.vector.tensor_copy(
+                out=s_dst[:, :, b, 0 : nw - sh], in_=s_src[:, 0 : 2 * WS, b, sh:nw]
+            )
+
+        state = {}
+
+        def presort(k):
+            wr = raw.tile([P, C * TAPS], BF16, tag="raw")
+            nc.sync.dma_start(
+                out=wr[:], in_=weight[k // WS, k % WS].rearrange("o c u v -> o (c u v)")
+            )
+            ws = st2.tile([P, C * TAPS], BF16, tag="st2", align_bytes=64)
+            src = wr[:].rearrange("o (p u e n) -> o n u p e", p=P, u=2, e=2, n=TAPS)
+            dst = ws[:].rearrange("o (n u p e) -> o n u p e", p=P, u=2, e=2, n=TAPS)
+            nv = TAPS - len(W_SCALAR_UNITS)
+            nc.vector.tensor_copy(out=dst[:, 0:nv], in_=src[:, 0:nv])
+            for n in W_SCALAR_UNITS:
+                nc.scalar.copy(out=dst[:, n], in_=src[:, n])
+            state[("ws", k)] = ws
+
+        def transposes(k):
+            ws32 = state[("ws", k)][:].bitcast(F32)
+            gw = grp.tile([P, TAPS * O * 4], BF16, align_bytes=64)
+            gw32 = gw[:].bitcast(F32).rearrange("p (n o u) -> p n o u", n=TAPS, o=O, u=2)
+            for n0 in range(0, TAPS, 2):
+                cnt = min(2, TAPS - n0)
+                pt = psum.tile([P, 2, 2, O], F32, tag="pt", bufs=4)
+                for i in range(cnt):
+                    for u in range(2):
+                        col = ((n0 + i) * 2 + u) * P
+                        nc.tensor.transpose(pt[:, i, u, :], ws32[:, col : col + P], ident_f[:])
+                nc.scalar.copy(
+                    out=gw32[:, n0 : n0 + cnt],
+                    in_=pt[:, 0:cnt].rearrange("p n u o -> p n o u"),
+                )
+            state[("gw", k)] = gw
+
+        def quantise(k):
+            gw = state[("gw", k)]
+            wc = wq.tile([P, TAPS * O], U32, align_bytes=64)
+            wsc = wq.tile([P, TAPS * O], U8, align_bytes=64)
+            big = 8 * O
+            nc.vector.quantize_mx(
+                out=wc[:, 0:big].bitcast(FP8X4), scales=wsc[:, 0:big], in_=gw[:, 0 : 4 * big]
+            )
+            nc.vector.quantize_mx(
+                out=wc[:, big : big + O].bitcast(FP8X4),
+                scales=wsc[:, big : big + O],
+                in_=gw[:, 4 * big : 4 * (big + O)],
+            )
+            state[("wc", k)] = (wc, wsc)
+
+        def multiply(k):
+            h, w = k // WS, k % WS
+            wc, wsc = state[("wc", k)]
+            acc0 = psum.tile([P, B * PIX], F32, tag="acc0")
+            accs = [acc0]
+            if w + K - 1 >= WS:
+                acc1 = psum.tile([P, B * PIX], F32, tag="acc1")
+                accs.append(acc1)
+            taps = [[n for n in range(TAPS) if (w + n % K) // WS == dj] for dj in range(len(accs))]
+            for b in range(B):
+                for n in range(TAPS):
+                    u, v = n // K, n % K
+                    ph, di = (h + u) % HS, (h + u) // HS
+                    q, dj = (w + v) % WS, (w + v) // WS
+                    cls = ph * WS + q
+                    scl = xs14 if di else xs4
+                    nc.tensor.matmul_mx(
+                        out=accs[dj][:, b * PIX : (b + 1) * PIX],
+                        lhsT=wc[:, n * O : (n + 1) * O].bitcast(FP8X4),
+                        lhsT_scale=wsc[:, n * O : (n + 1) * O],
+                        rhs=xc4[:, cls, b, di * NJ : di * NJ + PIX].bitcast(FP8X4),
+                        rhs_scale=scl[:, cls, b, :],
+                        start=(n == taps[dj][0]),
+                        stop=(n == taps[dj][-1]),
+                    )
+            state[("acc", k)] = accs
+
+        def finish(k):
+            h, w = k // WS, k % WS
+            accs = state[("acc", k)]
+            if w == 0:
+                planes = res.tile([P, WS, B * PIX], F32)
+                state[("planes", h)] = planes
+            planes = state[("planes", h)]
+            nc.scalar.activation(
+                out=planes[:, w, :], in_=accs[0][:], func=IDENT, bias=bias_sb[:, k : k + 1], scale=1.0
+            )
+            if len(accs) > 1:
+                pv = planes[:, w, :].rearrange("p (r j) -> p r j", j=NJ)
+                av = accs[1][:].rearrange("p (r j) -> p r j", j=NJ)
+                nc.vector.tensor_tensor(
+                    out=pv[:, :, 0 : NJ - 1], in0=pv[:, :, 0 : NJ - 1], in1=av[:, :, 1:NJ], op=ADD
+                )
+            if w == WS - 1:
+                ot = res.tile([P, B * PIX * WS], F32)
+                nc.gpsimd.tensor_scalar(
+                    out=ot[:].rearrange("p (x w) -> p x w", w=WS),
+                    in0=planes[:].rearrange("p w x -> p x w"),
+                    scalar1=1.0,
+                    scalar2=0.0,
+                    op0=MULT,
+                    op1=ADD,
+                )
+                for b in range(B):
+                    nc.sync.dma_start(
+                        out=out[b].rearrange("o (i h) z -> h o i z", h=HS)[h],
+                        in_=ot[:, b * PIX * WS : (b + 1) * PIX * WS].rearrange(
+                            "p (i z) -> p i z", z=W
+                        ),
+                    )
+
+        for step in range(NCLS + 4):
+            if step < NCLS:
+                presort(step)
+            if 0 <= step - 1 < NCLS:
+                transposes(step - 1)
+                quantise(step - 1)
+            if 0 <= step - 2 < NCLS:
+                multiply(step - 2)
+            if 0 <= step - 3 < NCLS:
+                finish(step - 3)

@@ -10,7 +10,6 @@ U32 = mybir.dt.uint32
 I32 = mybir.dt.int32
 FP8X4 = mybir.dt.float8_e4m3fn_x4
 ADD = mybir.AluOpType.add
-MULT = mybir.AluOpType.mult
 IDENT = mybir.ActivationFunctionType.Identity
 
 P = 128
@@ -24,20 +23,29 @@ PADPIX = PIX + NJ
 XROWS = 16
 XI = XROWS // HS
 NCHUNK = H // XROWS
+NX = B * NCHUNK
 FLOPS = 2 * B * O * H * W * C * TAPS
 
-X_SCALAR_PH = (2, 3)
-W_SCALAR_UNITS = (7, 8)
+NHEAD = 3
+GROUPS = 3
+
+
+def scalar_groups(k):
+    if k < NHEAD:
+        return GROUPS
+    return 1 if k % 2 == 1 else 0
 
 
 def tile_patternconv_t_kernel(tc, x, weight, bias, out):
     nc = tc.nc
     with ExitStack() as ctx:
         const = ctx.enter_context(tc.tile_pool(name="const", bufs=1))
-        raw = ctx.enter_context(tc.tile_pool(name="raw", bufs=6))
-        st2 = ctx.enter_context(tc.tile_pool(name="st2", bufs=3))
+        xraw = ctx.enter_context(tc.tile_pool(name="xraw", bufs=3))
+        wraw = ctx.enter_context(tc.tile_pool(name="wraw", bufs=4))
+        xgp = ctx.enter_context(tc.tile_pool(name="xgp", bufs=2))
+        wsp = ctx.enter_context(tc.tile_pool(name="wsp", bufs=3))
         grp = ctx.enter_context(tc.tile_pool(name="grp", bufs=2))
-        wq = ctx.enter_context(tc.tile_pool(name="wq", bufs=3))
+        wq = ctx.enter_context(tc.tile_pool(name="wq", bufs=4))
         res = ctx.enter_context(tc.tile_pool(name="res", bufs=2))
         psum = ctx.enter_context(tc.psum_pool(name="psum", bufs=2))
 
@@ -57,66 +65,81 @@ def tile_patternconv_t_kernel(tc, x, weight, bias, out):
         nc.vector.memset(
             xc[:].bitcast(I32).rearrange("p (g c) -> p g c", c=PADPIX)[:, :, PIX:PADPIX], 0
         )
-
         bias_rows = const.tile([P, P], BF16)
         nc.vector.memset(bias_rows[:], 0.0)
-        nc.sync.dma_start(out=bias_rows[0:NCLS, :], in_=bias.rearrange("h w o -> (h w) o"))
-        bias_ps = psum.tile([P, P], BF16, tag="pt", bufs=4)
-        nc.tensor.transpose(bias_ps[:], bias_rows[:], ident_b[:])
         bias_sb = const.tile([P, NCLS], F32)
-        nc.vector.tensor_copy(out=bias_sb[:], in_=bias_ps[:, 0:NCLS])
-
-        for b in range(B):
-            for ch in range(NCHUNK):
-                xr = raw.tile([P, 4, XROWS * W], BF16, tag="raw")
-                nc.sync.dma_start(
-                    out=xr[:],
-                    in_=x[b, :, ch * XROWS : (ch + 1) * XROWS, :].rearrange(
-                        "(p t) y z -> p t (y z)", t=4
-                    ),
-                )
-                xg = st2.tile([P, NCLS, XI * NJ * 4], BF16, tag="st2", align_bytes=64)
-                src = xr[:].rearrange(
-                    "p t (i a j q) -> p a q i j t", i=XI, a=HS, j=NJ, q=WS
-                )
-                dst = xg[:].rearrange(
-                    "p (a q) (i j t) -> p a q i j t", a=HS, q=WS, i=XI, j=NJ, t=4
-                )
-                for ph in range(HS):
-                    if ph in X_SCALAR_PH:
-                        for q in range(WS):
-                            nc.scalar.copy(out=dst[:, ph, q], in_=src[:, ph, q])
-                    else:
-                        nc.vector.tensor_copy(out=dst[:, ph], in_=src[:, ph])
-                cols = slice(ch * XI * NJ, (ch + 1) * XI * NJ)
-                for cls in range(NCLS):
-                    nc.vector.quantize_mx(
-                        out=xc4[:, cls, b, cols].bitcast(FP8X4),
-                        scales=xs4[:, cls, b, cols],
-                        in_=xg[:, cls, :],
-                    )
-            s_src = xs[:].bitcast(I32).rearrange("p (k b c) -> p k b c", k=NCLS, b=B)
-            s_dst = xs1[:].bitcast(I32).rearrange("p (k b c) -> p k b c", k=2 * WS, b=B)
-            nw = PIX // 4
-            sh = NJ // 4
-            nc.vector.tensor_copy(
-                out=s_dst[:, :, b, 0 : nw - sh], in_=s_src[:, 0 : 2 * WS, b, sh:nw]
-            )
 
         state = {}
 
-        def presort(k):
-            wr = raw.tile([P, C * TAPS], BF16, tag="raw")
+        def load_bias():
+            nc.sync.dma_start(out=bias_rows[0:NCLS, :], in_=bias.rearrange("h w o -> (h w) o"))
+
+        def spread_bias():
+            bias_ps = psum.tile([P, P], BF16, tag="pt", bufs=4)
+            nc.tensor.transpose(bias_ps[:], bias_rows[:], ident_b[:])
+            nc.vector.tensor_copy(out=bias_sb[:], in_=bias_ps[:, 0:NCLS])
+
+        def load_x(m):
+            b, ch = m // NCHUNK, m % NCHUNK
+            xr = xraw.tile([P, 4, XROWS * W], BF16)
+            for u in range(2):
+                nc.sync.dma_start(
+                    out=xr[:, 2 * u : 2 * u + 2, :],
+                    in_=x[
+                        b, 256 * u : 256 * (u + 1), ch * XROWS : (ch + 1) * XROWS, :
+                    ].rearrange("(p e) y z -> p e (y z)", e=2),
+                )
+            state[("xr", m)] = xr
+
+        def regroup_x(m):
+            xr = state[("xr", m)]
+            xg = xgp.tile([P, NCLS, XI * NJ * 4], BF16, align_bytes=64)
+            src = xr[:].rearrange("p t (i a j q) -> p a i j t q", i=XI, a=HS, j=NJ, q=WS)
+            dst = xg[:].rearrange(
+                "p (a q) (i j t) -> p a i j t q", a=HS, q=WS, i=XI, j=NJ, t=4
+            )
+            for ph in range(HS):
+                nc.vector.tensor_copy(out=dst[:, ph], in_=src[:, ph])
+            state[("xg", m)] = xg
+
+        def quantise_x(m):
+            b, ch = m // NCHUNK, m % NCHUNK
+            xg = state[("xg", m)]
+            cols = slice(ch * XI * NJ, (ch + 1) * XI * NJ)
+            for cls in range(NCLS):
+                nc.vector.quantize_mx(
+                    out=xc4[:, cls, b, cols].bitcast(FP8X4),
+                    scales=xs4[:, cls, b, cols],
+                    in_=xg[:, cls, :],
+                )
+            if ch == NCHUNK - 1:
+                s_src = xs[:].bitcast(I32).rearrange("p (k b c) -> p k b c", k=NCLS, b=B)
+                s_dst = xs1[:].bitcast(I32).rearrange("p (k b c) -> p k b c", k=2 * WS, b=B)
+                nw = PIX // 4
+                sh = NJ // 4
+                nc.vector.tensor_copy(
+                    out=s_dst[:, :, b, 0 : nw - sh], in_=s_src[:, 0 : 2 * WS, b, sh:nw]
+                )
+
+        def load_w(k):
+            wr = wraw.tile([P, C * TAPS], BF16)
             nc.sync.dma_start(
                 out=wr[:], in_=weight[k // WS, k % WS].rearrange("o c u v -> o (c u v)")
             )
-            ws = st2.tile([P, C * TAPS], BF16, tag="st2", align_bytes=64)
-            src = wr[:].rearrange("o (p u e n) -> o n u p e", p=P, u=2, e=2, n=TAPS)
-            dst = ws[:].rearrange("o (n u p e) -> o n u p e", p=P, u=2, e=2, n=TAPS)
-            nv = TAPS - len(W_SCALAR_UNITS)
-            nc.vector.tensor_copy(out=dst[:, 0:nv], in_=src[:, 0:nv])
-            for n in W_SCALAR_UNITS:
-                nc.scalar.copy(out=dst[:, n], in_=src[:, n])
+            state[("wr", k)] = wr
+
+        def sort_w(k):
+            wr = state[("wr", k)]
+            ws = wsp.tile([P, C * TAPS], BF16, align_bytes=64)
+            src = wr[:].rearrange("o (c n) -> o c n", n=TAPS)
+            dst = ws[:].rearrange("o (n c) -> o c n", n=TAPS)
+            ns = scalar_groups(k)
+            for g in range(GROUPS):
+                sl = slice(3 * g, 3 * g + 3)
+                if g >= GROUPS - ns:
+                    nc.scalar.copy(out=dst[:, :, sl], in_=src[:, :, sl])
+                else:
+                    nc.vector.tensor_copy(out=dst[:, :, sl], in_=src[:, :, sl])
             state[("ws", k)] = ws
 
         def transposes(k):
@@ -136,7 +159,7 @@ def tile_patternconv_t_kernel(tc, x, weight, bias, out):
                 )
             state[("gw", k)] = gw
 
-        def quantise(k):
+        def quantise_w(k):
             gw = state[("gw", k)]
             wc = wq.tile([P, TAPS * O], U32, align_bytes=64)
             wsc = wq.tile([P, TAPS * O], U8, align_bytes=64)
@@ -151,32 +174,33 @@ def tile_patternconv_t_kernel(tc, x, weight, bias, out):
             )
             state[("wc", k)] = (wc, wsc)
 
-        def multiply(k):
+        def multiply(k, b):
             h, w = k // WS, k % WS
             wc, wsc = state[("wc", k)]
-            acc0 = psum.tile([P, B * PIX], F32, tag="acc0")
-            accs = [acc0]
-            if w + K - 1 >= WS:
-                acc1 = psum.tile([P, B * PIX], F32, tag="acc1")
-                accs.append(acc1)
+            if b == 0:
+                acc0 = psum.tile([P, B * PIX], F32, tag="acc0")
+                accs = [acc0]
+                if w + K - 1 >= WS:
+                    acc1 = psum.tile([P, B * PIX], F32, tag="acc1")
+                    accs.append(acc1)
+                state[("acc", k)] = accs
+            accs = state[("acc", k)]
             taps = [[n for n in range(TAPS) if (w + n % K) // WS == dj] for dj in range(len(accs))]
-            for b in range(B):
-                for n in range(TAPS):
-                    u, v = n // K, n % K
-                    ph, di = (h + u) % HS, (h + u) // HS
-                    q, dj = (w + v) % WS, (w + v) // WS
-                    cls = ph * WS + q
-                    scl = xs14 if di else xs4
-                    nc.tensor.matmul_mx(
-                        out=accs[dj][:, b * PIX : (b + 1) * PIX],
-                        lhsT=wc[:, n * O : (n + 1) * O].bitcast(FP8X4),
-                        lhsT_scale=wsc[:, n * O : (n + 1) * O],
-                        rhs=xc4[:, cls, b, di * NJ : di * NJ + PIX].bitcast(FP8X4),
-                        rhs_scale=scl[:, cls, b, :],
-                        start=(n == taps[dj][0]),
-                        stop=(n == taps[dj][-1]),
-                    )
-            state[("acc", k)] = accs
+            for n in range(TAPS):
+                u, v = n // K, n % K
+                ph, di = (h + u) % HS, (h + u) // HS
+                q, dj = (w + v) % WS, (w + v) // WS
+                cls = ph * WS + q
+                scl = xs14 if di else xs4
+                nc.tensor.matmul_mx(
+                    out=accs[dj][:, b * PIX : (b + 1) * PIX],
+                    lhsT=wc[:, n * O : (n + 1) * O].bitcast(FP8X4),
+                    lhsT_scale=wsc[:, n * O : (n + 1) * O],
+                    rhs=xc4[:, cls, b, di * NJ : di * NJ + PIX].bitcast(FP8X4),
+                    rhs_scale=scl[:, cls, b, :],
+                    start=(n == taps[dj][0]),
+                    stop=(n == taps[dj][-1]),
+                )
 
         def finish(k):
             h, w = k // WS, k % WS
@@ -196,13 +220,9 @@ def tile_patternconv_t_kernel(tc, x, weight, bias, out):
                 )
             if w == WS - 1:
                 ot = res.tile([P, B * PIX * WS], F32)
-                nc.gpsimd.tensor_scalar(
+                nc.vector.tensor_copy(
                     out=ot[:].rearrange("p (x w) -> p x w", w=WS),
-                    in0=planes[:].rearrange("p w x -> p x w"),
-                    scalar1=1.0,
-                    scalar2=0.0,
-                    op0=MULT,
-                    op1=ADD,
+                    in_=planes[:].rearrange("p w x -> p x w"),
                 )
                 for b in range(B):
                     nc.sync.dma_start(
@@ -212,13 +232,52 @@ def tile_patternconv_t_kernel(tc, x, weight, bias, out):
                         ),
                     )
 
-        for step in range(NCLS + 4):
-            if step < NCLS:
-                presort(step)
-            if 0 <= step - 1 < NCLS:
-                transposes(step - 1)
-                quantise(step - 1)
-            if 0 <= step - 2 < NCLS:
-                multiply(step - 2)
-            if 0 <= step - 3 < NCLS:
-                finish(step - 3)
+        load_x(0)
+        load_w(0)
+        load_x(1)
+        load_bias()
+        load_x(2)
+        load_w(1)
+        spread_bias()
+        sort_w(0)
+        for m in range(NX + 1):
+            if m + 3 < NX:
+                load_x(m + 3)
+            if m in (1, 3, 5, 7):
+                load_w((m + 3) // 2)
+            if m < NX:
+                regroup_x(m)
+            if m >= 1:
+                quantise_x(m - 1)
+            if m == 1:
+                sort_w(1)
+                transposes(0)
+            if m == 3:
+                quantise_w(0)
+                sort_w(2)
+                transposes(1)
+            if m == 5:
+                quantise_w(1)
+                multiply(0, 0)
+                transposes(2)
+            if m == 6:
+                multiply(1, 0)
+            if m == 7:
+                quantise_w(2)
+
+        for s in range(NCLS + 2):
+            a = NHEAD + s
+            if a + 3 < NCLS:
+                load_w(a + 3)
+            if a < NCLS:
+                sort_w(a)
+            if NHEAD <= a - 1 < NCLS:
+                transposes(a - 1)
+            if NHEAD <= a - 2 < NCLS:
+                quantise_w(a - 2)
+            if s < NCLS:
+                if s >= 2:
+                    multiply(s, 0)
+                multiply(s, 1)
+            if 0 <= s - 1 < NCLS:
+                finish(s - 1)

@@ -26,7 +26,7 @@ NCHUNK = H // XROWS
 NX = B * NCHUNK
 FLOPS = 2 * B * O * H * W * C * TAPS
 
-NHEAD = 3
+NHEAD = 4
 GROUPS = 3
 
 
@@ -45,9 +45,10 @@ def tile_patternconv_t_kernel(tc, x, weight, bias, out):
         xgp = ctx.enter_context(tc.tile_pool(name="xgp", bufs=2))
         wsp = ctx.enter_context(tc.tile_pool(name="wsp", bufs=3))
         grp = ctx.enter_context(tc.tile_pool(name="grp", bufs=2))
-        wq = ctx.enter_context(tc.tile_pool(name="wq", bufs=4))
+        wq = ctx.enter_context(tc.tile_pool(name="wq", bufs=5))
         res = ctx.enter_context(tc.tile_pool(name="res", bufs=2))
         psum = ctx.enter_context(tc.psum_pool(name="psum", bufs=2))
+        ctx.enter_context(tc.manual_schedule())
 
         ident_f = const.tile([P, P], F32)
         make_identity(nc, ident_f[:])
@@ -71,13 +72,19 @@ def tile_patternconv_t_kernel(tc, x, weight, bias, out):
 
         state = {}
 
+        def hw(k):
+            return k // WS, WS - 1 - k % WS
+
         def load_bias():
             nc.sync.dma_start(out=bias_rows[0:NCLS, :], in_=bias.rearrange("h w o -> (h w) o"))
 
-        def spread_bias():
+        def bias_transpose():
             bias_ps = psum.tile([P, P], BF16, tag="pt", bufs=4)
             nc.tensor.transpose(bias_ps[:], bias_rows[:], ident_b[:])
-            nc.vector.tensor_copy(out=bias_sb[:], in_=bias_ps[:, 0:NCLS])
+            state["bias_ps"] = bias_ps
+
+        def bias_copy():
+            nc.vector.tensor_copy(out=bias_sb[:], in_=state["bias_ps"][:, 0:NCLS])
 
         def load_x(m):
             b, ch = m // NCHUNK, m % NCHUNK
@@ -122,25 +129,24 @@ def tile_patternconv_t_kernel(tc, x, weight, bias, out):
                 )
 
         def load_w(k):
+            h, w = hw(k)
             wr = wraw.tile([P, C * TAPS], BF16)
-            nc.sync.dma_start(
-                out=wr[:], in_=weight[k // WS, k % WS].rearrange("o c u v -> o (c u v)")
-            )
+            nc.sync.dma_start(out=wr[:], in_=weight[h, w].rearrange("o c u v -> o (c u v)"))
             state[("wr", k)] = wr
 
-        def sort_w(k):
-            wr = state[("wr", k)]
-            ws = wsp.tile([P, C * TAPS], BF16, align_bytes=64)
-            src = wr[:].rearrange("o (c n) -> o c n", n=TAPS)
-            dst = ws[:].rearrange("o (n c) -> o c n", n=TAPS)
+        def sort_w(k, groups):
+            if ("ws", k) not in state:
+                ws = wsp.tile([P, C * TAPS], BF16, align_bytes=64)
+                state[("ws", k)] = ws
+            src = state[("wr", k)][:].rearrange("o (c n) -> o c n", n=TAPS)
+            dst = state[("ws", k)][:].rearrange("o (n c) -> o c n", n=TAPS)
             ns = scalar_groups(k)
-            for g in range(GROUPS):
+            for g in groups:
                 sl = slice(3 * g, 3 * g + 3)
                 if g >= GROUPS - ns:
                     nc.scalar.copy(out=dst[:, :, sl], in_=src[:, :, sl])
                 else:
                     nc.vector.tensor_copy(out=dst[:, :, sl], in_=src[:, :, sl])
-            state[("ws", k)] = ws
 
         def transposes(k):
             ws32 = state[("ws", k)][:].bitcast(F32)
@@ -174,26 +180,33 @@ def tile_patternconv_t_kernel(tc, x, weight, bias, out):
             )
             state[("wc", k)] = (wc, wsc)
 
+        LAST = NCLS - 1
+
         def multiply(k, b):
-            h, w = k // WS, k % WS
+            h, w = hw(k)
             wc, wsc = state[("wc", k)]
             if b == 0:
                 acc0 = psum.tile([P, B * PIX], F32, tag="acc0")
                 accs = [acc0]
-                if w + K - 1 >= WS:
+                if w + K - 1 >= WS or k == LAST:
                     acc1 = psum.tile([P, B * PIX], F32, tag="acc1")
                     accs.append(acc1)
                 state[("acc", k)] = accs
             accs = state[("acc", k)]
-            taps = [[n for n in range(TAPS) if (w + n % K) // WS == dj] for dj in range(len(accs))]
+            ndj = 2 if w + K - 1 >= WS else 1
+            taps = [[n for n in range(TAPS) if (w + n % K) // WS == dj] for dj in range(ndj)]
             for n in range(TAPS):
                 u, v = n // K, n % K
                 ph, di = (h + u) % HS, (h + u) // HS
                 q, dj = (w + v) % WS, (w + v) // WS
                 cls = ph * WS + q
                 scl = xs14 if di else xs4
+                if k == LAST:
+                    dest = accs[b][:, 0:PIX]
+                else:
+                    dest = accs[dj][:, b * PIX : (b + 1) * PIX]
                 nc.tensor.matmul_mx(
-                    out=accs[dj][:, b * PIX : (b + 1) * PIX],
+                    out=dest,
                     lhsT=wc[:, n * O : (n + 1) * O].bitcast(FP8X4),
                     lhsT_scale=wsc[:, n * O : (n + 1) * O],
                     rhs=xc4[:, cls, b, di * NJ : di * NJ + PIX].bitcast(FP8X4),
@@ -202,29 +215,47 @@ def tile_patternconv_t_kernel(tc, x, weight, bias, out):
                     stop=(n == taps[dj][-1]),
                 )
 
-        def finish(k):
-            h, w = k // WS, k % WS
+        def evacuate(k):
+            h, w = hw(k)
             accs = state[("acc", k)]
-            if w == 0:
+            if w == WS - 1:
                 planes = res.tile([P, WS, B * PIX], F32)
                 state[("planes", h)] = planes
             planes = state[("planes", h)]
-            nc.scalar.activation(
-                out=planes[:, w, :], in_=accs[0][:], func=IDENT, bias=bias_sb[:, k : k + 1], scale=1.0
-            )
-            if len(accs) > 1:
+            bcol = bias_sb[:, h * WS + w : h * WS + w + 1]
+            if k == LAST:
+                for b in range(B):
+                    nc.scalar.activation(
+                        out=planes[:, w, b * PIX : (b + 1) * PIX],
+                        in_=accs[b][:, 0:PIX],
+                        func=IDENT,
+                        bias=bcol,
+                        scale=1.0,
+                    )
+            else:
+                nc.scalar.activation(
+                    out=planes[:, w, :], in_=accs[0][:], func=IDENT, bias=bcol, scale=1.0
+                )
+
+        def combine(k):
+            h, w = hw(k)
+            accs = state[("acc", k)]
+            planes = state[("planes", h)]
+            if w + K - 1 >= WS:
                 pv = planes[:, w, :].rearrange("p (r j) -> p r j", j=NJ)
                 av = accs[1][:].rearrange("p (r j) -> p r j", j=NJ)
                 nc.vector.tensor_tensor(
                     out=pv[:, :, 0 : NJ - 1], in0=pv[:, :, 0 : NJ - 1], in1=av[:, :, 1:NJ], op=ADD
                 )
-            if w == WS - 1:
+            if w == 0:
                 ot = res.tile([P, B * PIX * WS], F32)
-                nc.vector.tensor_copy(
-                    out=ot[:].rearrange("p (x w) -> p x w", w=WS),
-                    in_=planes[:].rearrange("p w x -> p x w"),
-                )
                 for b in range(B):
+                    nc.vector.tensor_copy(
+                        out=ot[:, b * PIX * WS : (b + 1) * PIX * WS].rearrange(
+                            "p (x w) -> p x w", w=WS
+                        ),
+                        in_=planes[:, :, b * PIX : (b + 1) * PIX].rearrange("p w x -> p x w"),
+                    )
                     nc.sync.dma_start(
                         out=out[b].rearrange("o (i h) z -> h o i z", h=HS)[h],
                         in_=ot[:, b * PIX * WS : (b + 1) * PIX * WS].rearrange(
@@ -232,52 +263,85 @@ def tile_patternconv_t_kernel(tc, x, weight, bias, out):
                         ),
                     )
 
+        ALLG = (0, 1, 2)
+
         load_x(0)
         load_w(0)
         load_x(1)
-        load_bias()
         load_x(2)
+        load_bias()
         load_w(1)
-        spread_bias()
-        sort_w(0)
-        for m in range(NX + 1):
-            if m + 3 < NX:
-                load_x(m + 3)
-            if m in (1, 3, 5, 7):
-                load_w((m + 3) // 2)
-            if m < NX:
-                regroup_x(m)
-            if m >= 1:
-                quantise_x(m - 1)
-            if m == 1:
-                sort_w(1)
-                transposes(0)
-            if m == 3:
-                quantise_w(0)
-                sort_w(2)
-                transposes(1)
-            if m == 5:
-                quantise_w(1)
-                multiply(0, 0)
-                transposes(2)
-            if m == 6:
-                multiply(1, 0)
-            if m == 7:
-                quantise_w(2)
+        bias_transpose()
+        sort_w(0, ALLG)
+        regroup_x(0)
+        load_x(3)
+        sort_w(1, ALLG)
+        transposes(0)
+        regroup_x(1)
+        load_x(4)
+        load_w(2)
+        quantise_x(0)
+        bias_copy()
+        regroup_x(2)
+        load_x(5)
+        quantise_x(1)
+        sort_w(2, ALLG)
+        transposes(1)
+        regroup_x(3)
+        load_x(6)
+        load_w(3)
+        quantise_x(2)
+        regroup_x(4)
+        load_x(7)
+        quantise_x(3)
+        load_w(4)
+        quantise_w(0)
+        multiply(0, 0)
+        sort_w(3, ALLG)
+        transposes(2)
+        regroup_x(5)
+        quantise_x(4)
+        load_w(5)
+        regroup_x(6)
+        quantise_x(5)
+        quantise_w(1)
+        multiply(1, 0)
+        transposes(3)
+        regroup_x(7)
+        quantise_x(6)
+        load_w(6)
+        quantise_x(7)
+        quantise_w(2)
+        quantise_w(3)
 
-        for s in range(NCLS + 2):
+        pending = []
+        for s in range(NCLS):
             a = NHEAD + s
             if a + 3 < NCLS:
                 load_w(a + 3)
+            for k in pending:
+                evacuate(k)
             if a < NCLS:
-                sort_w(a)
-            if NHEAD <= a - 1 < NCLS:
-                transposes(a - 1)
+                sort_w(a, (0,))
             if NHEAD <= a - 2 < NCLS:
                 quantise_w(a - 2)
-            if s < NCLS:
-                if s >= 2:
-                    multiply(s, 0)
-                multiply(s, 1)
-            if 0 <= s - 1 < NCLS:
-                finish(s - 1)
+            for k in pending:
+                combine(k)
+            pending = []
+            if s == 0:
+                multiply(0, 1)
+                multiply(1, 1)
+                pending = [0, 1]
+            elif s + 1 < NCLS:
+                pending = [s + 1]
+                if s + 2 == LAST:
+                    pending.append(LAST)
+                if s + 1 == LAST:
+                    pending = []
+                for k in pending:
+                    multiply(k, 0)
+                    multiply(k, 1)
+            if a < NCLS:
+                sort_w(a, (1, 2))
+            if NHEAD <= a - 1 < NCLS:
+                transposes(a - 1)

@@ -30,10 +30,7 @@ NHEAD = 4
 GROUPS = 3
 
 
-def scalar_groups(k):
-    if k < NHEAD:
-        return GROUPS
-    return 1 if k % 2 == 1 else 0
+SPLIT = 192
 
 
 def tile_patternconv_t_kernel(tc, x, weight, bias, out):
@@ -140,13 +137,15 @@ def tile_patternconv_t_kernel(tc, x, weight, bias, out):
                 state[("ws", k)] = ws
             src = state[("wr", k)][:].rearrange("o (c n) -> o c n", n=TAPS)
             dst = state[("ws", k)][:].rearrange("o (n c) -> o c n", n=TAPS)
-            ns = scalar_groups(k)
             for g in groups:
                 sl = slice(3 * g, 3 * g + 3)
-                if g >= GROUPS - ns:
+                if k < NHEAD:
                     nc.scalar.copy(out=dst[:, :, sl], in_=src[:, :, sl])
-                else:
+                elif g < GROUPS - 1:
                     nc.vector.tensor_copy(out=dst[:, :, sl], in_=src[:, :, sl])
+                else:
+                    nc.vector.tensor_copy(out=dst[:, 0:SPLIT, sl], in_=src[:, 0:SPLIT, sl])
+                    nc.scalar.copy(out=dst[:, SPLIT:C, sl], in_=src[:, SPLIT:C, sl])
 
         def transposes(k):
             ws32 = state[("ws", k)][:].bitcast(F32)

@@ -24,6 +24,9 @@ XROWS = 16
 XI = XROWS // HS
 NCHUNK = H // XROWS
 NX = B * NCHUNK
+LOADS = [(0, 0, 8), (0, 8, 8)] + [
+    (b, r, XROWS) for b in range(B) for r in range(0, H, XROWS) if (b, r) != (0, 0)
+]
 FLOPS = 2 * B * O * H * W * C * TAPS
 
 NHEAD = 4
@@ -83,28 +86,33 @@ def tile_patternconv_t_kernel(tc, x, weight, bias, out):
         def bias_copy():
             nc.vector.tensor_copy(out=bias_sb[:], in_=state["bias_ps"][:, 0:NCLS])
 
-        def load_x(m):
-            b, ch = m // NCHUNK, m % NCHUNK
+        def load_x(l):
+            b, r0, nr = LOADS[l]
             xr = xraw.tile([P, 4, XROWS * W], BF16)
             for u in range(2):
                 nc.sync.dma_start(
-                    out=xr[:, 2 * u : 2 * u + 2, :],
-                    in_=x[
-                        b, 256 * u : 256 * (u + 1), ch * XROWS : (ch + 1) * XROWS, :
-                    ].rearrange("(p e) y z -> p e (y z)", e=2),
+                    out=xr[:, 2 * u : 2 * u + 2, 0 : nr * W],
+                    in_=x[b, 256 * u : 256 * (u + 1), r0 : r0 + nr, :].rearrange(
+                        "(p e) y z -> p e (y z)", e=2
+                    ),
                 )
-            state[("xr", m)] = xr
+            state[("xr", l)] = xr
 
-        def regroup_x(m):
-            xr = state[("xr", m)]
-            xg = xgp.tile([P, NCLS, XI * NJ * 4], BF16, align_bytes=64)
-            src = xr[:].rearrange("p t (i a j q) -> p a i j t q", i=XI, a=HS, j=NJ, q=WS)
-            dst = xg[:].rearrange(
-                "p (a q) (i j t) -> p a i j t q", a=HS, q=WS, i=XI, j=NJ, t=4
+        def regroup_x(l):
+            b, r0, nr = LOADS[l]
+            m = b * NCHUNK + r0 // XROWS
+            if r0 % XROWS == 0:
+                xg = xgp.tile([P, NCLS, XI * NJ * 4], BF16, align_bytes=64)
+                state[("xg", m)] = xg
+            i0, ni = (r0 % XROWS) // HS, nr // HS
+            src = state[("xr", l)][:, :, 0 : nr * W].rearrange(
+                "p t (i a j q) -> p a i j t q", i=ni, a=HS, j=NJ, q=WS
+            )
+            dst = state[("xg", m)][:, :, i0 * NJ * 4 : (i0 + ni) * NJ * 4].rearrange(
+                "p (a q) (i j t) -> p a i j t q", a=HS, q=WS, i=ni, j=NJ, t=4
             )
             for ph in range(HS):
                 nc.vector.tensor_copy(out=dst[:, ph], in_=src[:, ph])
-            state[("xg", m)] = xg
 
         def quantise_x(m):
             b, ch = m // NCHUNK, m % NCHUNK
@@ -168,15 +176,12 @@ def tile_patternconv_t_kernel(tc, x, weight, bias, out):
             gw = state[("gw", k)]
             wc = wq.tile([P, TAPS * O], U32, align_bytes=64)
             wsc = wq.tile([P, TAPS * O], U8, align_bytes=64)
-            big = 8 * O
-            nc.vector.quantize_mx(
-                out=wc[:, 0:big].bitcast(FP8X4), scales=wsc[:, 0:big], in_=gw[:, 0 : 4 * big]
-            )
-            nc.vector.quantize_mx(
-                out=wc[:, big : big + O].bitcast(FP8X4),
-                scales=wsc[:, big : big + O],
-                in_=gw[:, 4 * big : 4 * (big + O)],
-            )
+            for n0, n1 in ((0, 4), (4, 8), (8, 9)):
+                nc.vector.quantize_mx(
+                    out=wc[:, n0 * O : n1 * O].bitcast(FP8X4),
+                    scales=wsc[:, n0 * O : n1 * O],
+                    in_=gw[:, 4 * n0 * O : 4 * n1 * O],
+                )
             state[("wc", k)] = (wc, wsc)
 
         LAST = NCLS - 1
@@ -187,7 +192,7 @@ def tile_patternconv_t_kernel(tc, x, weight, bias, out):
             if b == 0:
                 acc0 = psum.tile([P, B * PIX], F32, tag="acc0")
                 accs = [acc0]
-                if w + K - 1 >= WS or k == LAST:
+                if w + K - 1 >= WS:
                     acc1 = psum.tile([P, B * PIX], F32, tag="acc1")
                     accs.append(acc1)
                 state[("acc", k)] = accs
@@ -200,12 +205,8 @@ def tile_patternconv_t_kernel(tc, x, weight, bias, out):
                 q, dj = (w + v) % WS, (w + v) // WS
                 cls = ph * WS + q
                 scl = xs14 if di else xs4
-                if k == LAST:
-                    dest = accs[b][:, 0:PIX]
-                else:
-                    dest = accs[dj][:, b * PIX : (b + 1) * PIX]
                 nc.tensor.matmul_mx(
-                    out=dest,
+                    out=accs[dj][:, b * PIX : (b + 1) * PIX],
                     lhsT=wc[:, n * O : (n + 1) * O].bitcast(FP8X4),
                     lhsT_scale=wsc[:, n * O : (n + 1) * O],
                     rhs=xc4[:, cls, b, di * NJ : di * NJ + PIX].bitcast(FP8X4),
@@ -222,19 +223,9 @@ def tile_patternconv_t_kernel(tc, x, weight, bias, out):
                 state[("planes", h)] = planes
             planes = state[("planes", h)]
             bcol = bias_sb[:, h * WS + w : h * WS + w + 1]
-            if k == LAST:
-                for b in range(B):
-                    nc.scalar.activation(
-                        out=planes[:, w, b * PIX : (b + 1) * PIX],
-                        in_=accs[b][:, 0:PIX],
-                        func=IDENT,
-                        bias=bcol,
-                        scale=1.0,
-                    )
-            else:
-                nc.scalar.activation(
-                    out=planes[:, w, :], in_=accs[0][:], func=IDENT, bias=bcol, scale=1.0
-                )
+            nc.scalar.activation(
+                out=planes[:, w, :], in_=accs[0][:], func=IDENT, bias=bcol, scale=1.0
+            )
 
         def combine(k):
             h, w = hw(k)
@@ -262,51 +253,101 @@ def tile_patternconv_t_kernel(tc, x, weight, bias, out):
                         ),
                     )
 
+        QPIX = PIX // 2
+
+        def multiply_piece(pc):
+            h, w = hw(LAST)
+            b, c0 = pc // 2, (pc % 2) * QPIX
+            wc, wsc = state[("wc", LAST)]
+            acc = psum.tile([P, B * PIX], F32, tag=("acc0" if pc in (0, 3) else "acc1"))
+            for n in range(TAPS):
+                u, v = n // K, n % K
+                ph, di = (h + u) % HS, (h + u) // HS
+                cls = ph * WS + w + v
+                scl = xs14 if di else xs4
+                nc.tensor.matmul_mx(
+                    out=acc[:, 0:QPIX],
+                    lhsT=wc[:, n * O : (n + 1) * O].bitcast(FP8X4),
+                    lhsT_scale=wsc[:, n * O : (n + 1) * O],
+                    rhs=xc4[:, cls, b, di * NJ + c0 : di * NJ + c0 + QPIX].bitcast(FP8X4),
+                    rhs_scale=scl[:, cls, b, c0 : c0 + QPIX],
+                    start=(n == 0),
+                    stop=(n == TAPS - 1),
+                )
+            state[("piece", pc)] = acc
+
+        def finish_piece(pc):
+            h, w = hw(LAST)
+            b, c0 = pc // 2, pc * QPIX
+            planes = state[("planes", h)]
+            if pc == 0:
+                ot = res.tile([P, B * PIX * WS], F32)
+                state["ot_last"] = ot
+            ot = state["ot_last"]
+            nc.scalar.activation(
+                out=planes[:, w, c0 : c0 + QPIX],
+                in_=state[("piece", pc)][:, 0:QPIX],
+                func=IDENT,
+                bias=bias_sb[:, h * WS + w : h * WS + w + 1],
+                scale=1.0,
+            )
+            nc.vector.tensor_copy(
+                out=ot[:, c0 * WS : (c0 + QPIX) * WS].rearrange("p (x w) -> p x w", w=WS),
+                in_=planes[:, :, c0 : c0 + QPIX].rearrange("p w x -> p x w"),
+            )
+            i0 = (pc % 2) * (NI // 2)
+            nc.sync.dma_start(
+                out=out[b].rearrange("o (i h) z -> h o i z", h=HS)[h][:, i0 : i0 + NI // 2, :],
+                in_=ot[:, c0 * WS : (c0 + QPIX) * WS].rearrange("p (i z) -> p i z", z=W),
+            )
+
         ALLG = (0, 1, 2)
 
         load_x(0)
-        load_w(0)
         load_x(1)
+        load_w(0)
         load_x(2)
-        load_bias()
-        load_w(1)
-        bias_transpose()
         sort_w(0, ALLG)
         regroup_x(0)
         load_x(3)
-        sort_w(1, ALLG)
-        transposes(0)
+        load_bias()
+        load_w(1)
+        bias_transpose()
         regroup_x(1)
         load_x(4)
+        sort_w(1, ALLG)
+        transposes(0)
+        regroup_x(2)
+        load_x(5)
         load_w(2)
         quantise_x(0)
         bias_copy()
-        regroup_x(2)
-        load_x(5)
+        regroup_x(3)
+        load_x(6)
         quantise_x(1)
         sort_w(2, ALLG)
         transposes(1)
-        regroup_x(3)
-        load_x(6)
-        load_w(3)
-        quantise_x(2)
         regroup_x(4)
         load_x(7)
+        load_w(3)
+        quantise_x(2)
+        regroup_x(5)
+        load_x(8)
         quantise_x(3)
         load_w(4)
         quantise_w(0)
         multiply(0, 0)
         sort_w(3, ALLG)
         transposes(2)
-        regroup_x(5)
+        regroup_x(6)
         quantise_x(4)
         load_w(5)
-        regroup_x(6)
+        regroup_x(7)
         quantise_x(5)
         quantise_w(1)
         multiply(1, 0)
         transposes(3)
-        regroup_x(7)
+        regroup_x(8)
         quantise_x(6)
         load_w(6)
         quantise_x(7)
@@ -314,7 +355,7 @@ def tile_patternconv_t_kernel(tc, x, weight, bias, out):
         quantise_w(3)
 
         pending = []
-        for s in range(NCLS):
+        for s in range(LAST - 1):
             a = NHEAD + s
             if a + 3 < NCLS:
                 load_w(a + 3)
@@ -331,16 +372,19 @@ def tile_patternconv_t_kernel(tc, x, weight, bias, out):
                 multiply(0, 1)
                 multiply(1, 1)
                 pending = [0, 1]
-            elif s + 1 < NCLS:
+            elif s + 1 < LAST:
                 pending = [s + 1]
-                if s + 2 == LAST:
-                    pending.append(LAST)
-                if s + 1 == LAST:
-                    pending = []
-                for k in pending:
-                    multiply(k, 0)
-                    multiply(k, 1)
+                multiply(s + 1, 0)
+                multiply(s + 1, 1)
             if a < NCLS:
                 sort_w(a, (1, 2))
             if NHEAD <= a - 1 < NCLS:
                 transposes(a - 1)
+
+        for pc in range(3):
+            multiply_piece(pc)
+        evacuate(LAST - 1)
+        combine(LAST - 1)
+        multiply_piece(3)
+        for pc in range(4):
+            finish_piece(pc)

@@ -48,7 +48,6 @@ def tile_patternconv_t_kernel(tc, x, weight, bias, out):
         wq = ctx.enter_context(tc.tile_pool(name="wq", bufs=5))
         res = ctx.enter_context(tc.tile_pool(name="res", bufs=2))
         psum = ctx.enter_context(tc.psum_pool(name="psum", bufs=2))
-        ctx.enter_context(tc.manual_schedule())
 
         ident_f = const.tile([P, P], F32)
         make_identity(nc, ident_f[:])

@@ -154,11 +154,14 @@ def tile_patternconv_t_kernel(tc, x, weight, bias, out):
                     nc.vector.tensor_copy(out=dst[:, 0:SPLIT, sl], in_=src[:, 0:SPLIT, sl])
                     nc.scalar.copy(out=dst[:, SPLIT:C, sl], in_=src[:, SPLIT:C, sl])
 
-        def transposes(k):
+        def transposes(k, first=0, last=TAPS):
             ws32 = state[("ws", k)][:].bitcast(F32)
-            gw = grp.tile([P, TAPS * O * 4], BF16, align_bytes=64)
+            if first == 0:
+                gw = grp.tile([P, TAPS * O * 4], BF16, align_bytes=64)
+                state[("gw", k)] = gw
+            gw = state[("gw", k)]
             gw32 = gw[:].bitcast(F32).rearrange("p (n o u) -> p n o u", n=TAPS, o=O, u=2)
-            for n0 in range(0, TAPS, 2):
+            for n0 in range(first, last, 2):
                 cnt = min(2, TAPS - n0)
                 pt = psum.tile([P, 2, 2, O], F32, tag="pt", bufs=4)
                 for i in range(cnt):
@@ -169,7 +172,6 @@ def tile_patternconv_t_kernel(tc, x, weight, bias, out):
                     out=gw32[:, n0 : n0 + cnt],
                     in_=pt[:, 0:cnt].rearrange("p n u o -> p n o u"),
                 )
-            state[("gw", k)] = gw
 
         def quantise_w(k):
             gw = state[("gw", k)]
@@ -353,6 +355,8 @@ def tile_patternconv_t_kernel(tc, x, weight, bias, out):
         quantise_w(2)
         quantise_w(3)
 
+        ctx.enter_context(tc.manual_schedule(engines={mybir.EngineType.PE}))
+        TCUT = 4
         pending = []
         for s in range(LAST - 1):
             a = NHEAD + s
@@ -367,6 +371,7 @@ def tile_patternconv_t_kernel(tc, x, weight, bias, out):
             for k in pending:
                 combine(k)
             pending = []
+            turn = NHEAD <= a - 1 < NCLS
             if s == 0:
                 multiply(0, 1)
                 multiply(1, 1)
@@ -374,11 +379,13 @@ def tile_patternconv_t_kernel(tc, x, weight, bias, out):
             elif s + 1 < LAST:
                 pending = [s + 1]
                 multiply(s + 1, 0)
+                if turn:
+                    transposes(a - 1, 0, TCUT)
                 multiply(s + 1, 1)
             if a < NCLS:
                 sort_w(a, (1, 2))
-            if NHEAD <= a - 1 < NCLS:
-                transposes(a - 1)
+            if turn:
+                transposes(a - 1, TCUT, TAPS)
 
         for pc in range(3):
             multiply_piece(pc)

@@ -353,7 +353,6 @@ def tile_patternconv_t_kernel(tc, x, weight, bias, out):
         load_w(6)
         quantise_x(7)
         quantise_w(2)
-        quantise_w(3)
 
         ctx.enter_context(tc.manual_schedule(engines={mybir.EngineType.PE}))
         TCUT = 4
@@ -384,6 +383,8 @@ def tile_patternconv_t_kernel(tc, x, weight, bias, out):
                 multiply(s + 1, 1)
             if a < NCLS:
                 sort_w(a, (1, 2))
+            if s == 0:
+                quantise_w(NHEAD - 1)
             if turn:
                 transposes(a - 1, TCUT, TAPS)
 

@@ -40,7 +40,7 @@ def tile_patternconv_t_kernel(tc, x, weight, bias, out):
     nc = tc.nc
     with ExitStack() as ctx:
         const = ctx.enter_context(tc.tile_pool(name="const", bufs=1))
-        xraw = ctx.enter_context(tc.tile_pool(name="xraw", bufs=3))
+        xraw = ctx.enter_context(tc.tile_pool(name="xraw", bufs=4))
         wraw = ctx.enter_context(tc.tile_pool(name="wraw", bufs=4))
         xgp = ctx.enter_context(tc.tile_pool(name="xgp", bufs=2))
         wsp = ctx.enter_context(tc.tile_pool(name="wsp", bufs=3))
@@ -239,19 +239,15 @@ def tile_patternconv_t_kernel(tc, x, weight, bias, out):
                     out=pv[:, :, 0 : NJ - 1], in0=pv[:, :, 0 : NJ - 1], in1=av[:, :, 1:NJ], op=ADD
                 )
             if w == 0:
-                ot = res.tile([P, B * PIX * WS], F32)
                 for b in range(B):
+                    ot = res.tile([P, PIX * WS], F32, bufs=3)
                     nc.vector.tensor_copy(
-                        out=ot[:, b * PIX * WS : (b + 1) * PIX * WS].rearrange(
-                            "p (x w) -> p x w", w=WS
-                        ),
+                        out=ot[:].rearrange("p (x w) -> p x w", w=WS),
                         in_=planes[:, :, b * PIX : (b + 1) * PIX].rearrange("p w x -> p x w"),
                     )
                     nc.sync.dma_start(
                         out=out[b].rearrange("o (i h) z -> h o i z", h=HS)[h],
-                        in_=ot[:, b * PIX * WS : (b + 1) * PIX * WS].rearrange(
-                            "p (i z) -> p i z", z=W
-                        ),
+                        in_=ot[:].rearrange("p (i z) -> p i z", z=W),
                     )
 
         QPIX = PIX // 2
@@ -281,10 +277,11 @@ def tile_patternconv_t_kernel(tc, x, weight, bias, out):
             h, w = hw(LAST)
             b, c0 = pc // 2, pc * QPIX
             planes = state[("planes", h)]
-            if pc == 0:
-                ot = res.tile([P, B * PIX * WS], F32)
+            if pc % 2 == 0:
+                ot = res.tile([P, PIX * WS], F32, bufs=3)
                 state["ot_last"] = ot
             ot = state["ot_last"]
+            o0 = (pc % 2) * QPIX * WS
             nc.scalar.activation(
                 out=planes[:, w, c0 : c0 + QPIX],
                 in_=state[("piece", pc)][:, 0:QPIX],
@@ -293,13 +290,13 @@ def tile_patternconv_t_kernel(tc, x, weight, bias, out):
                 scale=1.0,
             )
             nc.vector.tensor_copy(
-                out=ot[:, c0 * WS : (c0 + QPIX) * WS].rearrange("p (x w) -> p x w", w=WS),
+                out=ot[:, o0 : o0 + QPIX * WS].rearrange("p (x w) -> p x w", w=WS),
                 in_=planes[:, :, c0 : c0 + QPIX].rearrange("p w x -> p x w"),
             )
             i0 = (pc % 2) * (NI // 2)
             nc.sync.dma_start(
                 out=out[b].rearrange("o (i h) z -> h o i z", h=HS)[h][:, i0 : i0 + NI // 2, :],
-                in_=ot[:, c0 * WS : (c0 + QPIX) * WS].rearrange("p (i z) -> p i z", z=W),
+                in_=ot[:, o0 : o0 + QPIX * WS].rearrange("p (i z) -> p i z", z=W),
             )
 
         ALLG = (0, 1, 2)

from contextlib import ExitStack

import concourse.mybir as mybir
from concourse.masks import make_identity

F32 = mybir.dt.float32
BF16 = mybir.dt.bfloat16
U8 = mybir.dt.uint8
U32 = mybir.dt.uint32
I32 = mybir.dt.int32
FP8X4 = mybir.dt.float8_e4m3fn_x4
ADD = mybir.AluOpType.add
IDENT = mybir.ActivationFunctionType.Identity

P = 128
B, C, H, W, O = 2, 512, 64, 64, 128
HS, WS, K = 4, 4, 3
NI, NJ = H // HS, W // WS
TAPS = K * K
NCLS = HS * WS
PIX = NI * NJ
PADPIX = PIX + NJ
XROWS = 16
XI = XROWS // HS
NCHUNK = H // XROWS
NX = B * NCHUNK
LOADS = [(0, 0, 8), (0, 8, 8)] + [
    (b, r, XROWS) for b in range(B) for r in range(0, H, XROWS) if (b, r) != (0, 0)
]
FLOPS = 2 * B * O * H * W * C * TAPS

NHEAD = 4
GROUPS = 3


SPLIT = 192


def tile_patternconv_t_kernel(tc, x, weight, bias, out):
    nc = tc.nc
    with ExitStack() as ctx:
        const = ctx.enter_context(tc.tile_pool(name="const", bufs=1))
        xraw = ctx.enter_context(tc.tile_pool(name="xraw", bufs=4))
        wraw = ctx.enter_context(tc.tile_pool(name="wraw", bufs=4))
        xgp = ctx.enter_context(tc.tile_pool(name="xgp", bufs=2))
        wsp = ctx.enter_context(tc.tile_pool(name="wsp", bufs=3))
        grp = ctx.enter_context(tc.tile_pool(name="grp", bufs=2))
        wq = ctx.enter_context(tc.tile_pool(name="wq", bufs=5))
        res = ctx.enter_context(tc.tile_pool(name="res", bufs=2))
        psum = ctx.enter_context(tc.psum_pool(name="psum", bufs=2))

        ident_f = const.tile([P, P], F32)
        make_identity(nc, ident_f[:])
        ident_b = const.tile([P, P], BF16)
        make_identity(nc, ident_b[:])

        xc = const.tile([P, NCLS * B * PADPIX], U32, align_bytes=64)
        xs = const.tile([P, NCLS * B * PIX], U8, align_bytes=64)
        xs1 = const.tile([P, 2 * WS * B * PIX], U8, align_bytes=64)
        xc4 = xc[:].rearrange("p (k b c) -> p k b c", k=NCLS, b=B)
        xs4 = xs[:].rearrange("p (k b c) -> p k b c", k=NCLS, b=B)
        xs14 = xs1[:].rearrange("p (k b c) -> p k b c", k=2 * WS, b=B)
        nc.vector.memset(xs[:].bitcast(I32), 0)
        nc.vector.memset(xs1[:].bitcast(I32), 0)
        nc.vector.memset(
            xc[:].bitcast(I32).rearrange("p (g c) -> p g c", c=PADPIX)[:, :, PIX:PADPIX], 0
        )
        bias_rows = const.tile([P, P], BF16)
        nc.vector.memset(bias_rows[:], 0.0)
        bias_sb = const.tile([P, NCLS], F32)

        state = {}

        def hw(k):
            return k // WS, WS - 1 - k % WS

        def load_bias():
            nc.sync.dma_start(out=bias_rows[0:NCLS, :], in_=bias.rearrange("h w o -> (h w) o"))

        def bias_transpose():
            bias_ps = psum.tile([P, P], BF16, tag="pt", bufs=4)
            nc.tensor.transpose(bias_ps[:], bias_rows[:], ident_b[:])
            state["bias_ps"] = bias_ps

        def bias_copy():
            nc.vector.tensor_copy(out=bias_sb[:], in_=state["bias_ps"][:, 0:NCLS])

        def load_x(l):
            b, r0, nr = LOADS[l]
            xr = xraw.tile([P, 4, XROWS * W], BF16)
            for u in range(2):
                nc.sync.dma_start(
                    out=xr[:, 2 * u : 2 * u + 2, 0 : nr * W],
                    in_=x[b, 256 * u : 256 * (u + 1), r0 : r0 + nr, :].rearrange(
                        "(p e) y z -> p e (y z)", e=2
                    ),
                )
            state[("xr", l)] = xr

        def regroup_x(l):
            b, r0, nr = LOADS[l]
            m = b * NCHUNK + r0 // XROWS
            if r0 % XROWS == 0:
                xg = xgp.tile([P, NCLS, XI * NJ * 4], BF16, align_bytes=64)
                state[("xg", m)] = xg
            i0, ni = (r0 % XROWS) // HS, nr // HS
            src = state[("xr", l)][:, :, 0 : nr * W].rearrange(
                "p t (i a j q) -> p a i j t q", i=ni, a=HS, j=NJ, q=WS
            )
            dst = state[("xg", m)][:, :, i0 * NJ * 4 : (i0 + ni) * NJ * 4].rearrange(
                "p (a q) (i j t) -> p a i j t q", a=HS, q=WS, i=ni, j=NJ, t=4
            )
            for ph in range(HS):
                nc.vector.tensor_copy(out=dst[:, ph], in_=src[:, ph])

        def quantise_x(m):
            b, ch = m // NCHUNK, m % NCHUNK
            xg = state[("xg", m)]
            cols = slice(ch * XI * NJ, (ch + 1) * XI * NJ)
            for cls in range(NCLS):
                nc.vector.quantize_mx(
                    out=xc4[:, cls, b, cols].bitcast(FP8X4),
                    scales=xs4[:, cls, b, cols],
                    in_=xg[:, cls, :],
                )
            if ch == NCHUNK - 1:
                s_src = xs[:].bitcast(I32).rearrange("p (k b c) -> p k b c", k=NCLS, b=B)
                s_dst = xs1[:].bitcast(I32).rearrange("p (k b c) -> p k b c", k=2 * WS, b=B)
                nw = PIX // 4
                sh = NJ // 4
                nc.vector.tensor_copy(
                    out=s_dst[:, :, b, 0 : nw - sh], in_=s_src[:, 0 : 2 * WS, b, sh:nw]
                )

        def load_w(k):
            h, w = hw(k)
            wr = wraw.tile([P, C * TAPS], BF16)
            nc.sync.dma_start(out=wr[:], in_=weight[h, w].rearrange("o c u v -> o (c u v)"))
            state[("wr", k)] = wr

        def sort_w(k, groups):
            if ("ws", k) not in state:
                ws = wsp.tile([P, C * TAPS], BF16, align_bytes=64)
                state[("ws", k)] = ws
            src = state[("wr", k)][:].rearrange("o (c n) -> o c n", n=TAPS)
            dst = state[("ws", k)][:].rearrange("o (n c) -> o c n", n=TAPS)
            for g in groups:
                sl = slice(3 * g, 3 * g + 3)
                if k < NHEAD:
                    nc.scalar.copy(out=dst[:, :, sl], in_=src[:, :, sl])
                elif g < GROUPS - 1:
                    nc.vector.tensor_copy(out=dst[:, :, sl], in_=src[:, :, sl])
                else:
                    nc.vector.tensor_copy(out=dst[:, 0:SPLIT, sl], in_=src[:, 0:SPLIT, sl])
                    nc.scalar.copy(out=dst[:, SPLIT:C, sl], in_=src[:, SPLIT:C, sl])

        def transposes(k, first=0, last=TAPS):
            ws32 = state[("ws", k)][:].bitcast(F32)
            if first == 0:
                gw = grp.tile([P, TAPS * O * 4], BF16, align_bytes=64)
                state[("gw", k)] = gw
            gw = state[("gw", k)]
            gw32 = gw[:].bitcast(F32).rearrange("p (n o u) -> p n o u", n=TAPS, o=O, u=2)
            for n0 in range(first, last, 2):
                cnt = min(2, TAPS - n0)
                pt = psum.tile([P, 2, 2, O], F32, tag="pt", bufs=4)
                for i in range(cnt):
                    for u in range(2):
                        col = ((n0 + i) * 2 + u) * P
                        nc.tensor.transpose(pt[:, i, u, :], ws32[:, col : col + P], ident_f[:])
                nc.scalar.copy(
                    out=gw32[:, n0 : n0 + cnt],
                    in_=pt[:, 0:cnt].rearrange("p n u o -> p n o u"),
                )

        def quantise_w(k):
            gw = state[("gw", k)]
            wc = wq.tile([P, TAPS * O], U32, align_bytes=64)
            wsc = wq.tile([P, TAPS * O], U8, align_bytes=64)
            for n0, n1 in ((0, 4), (4, 8), (8, 9)):
                nc.vector.quantize_mx(
                    out=wc[:, n0 * O : n1 * O].bitcast(FP8X4),
                    scales=wsc[:, n0 * O : n1 * O],
                    in_=gw[:, 4 * n0 * O : 4 * n1 * O],
                )
            state[("wc", k)] = (wc, wsc)

        LAST = NCLS - 1

        def multiply(k, b):
            h, w = hw(k)
            wc, wsc = state[("wc", k)]
            if b == 0:
                acc0 = psum.tile([P, B * PIX], F32, tag="acc0")
                accs = [acc0]
                if w + K - 1 >= WS:
                    acc1 = psum.tile([P, B * PIX], F32, tag="acc1")
                    accs.append(acc1)
                state[("acc", k)] = accs
            accs = state[("acc", k)]
            ndj = 2 if w + K - 1 >= WS else 1
            taps = [[n for n in range(TAPS) if (w + n % K) // WS == dj] for dj in range(ndj)]
            for n in range(TAPS):
                u, v = n // K, n % K
                ph, di = (h + u) % HS, (h + u) // HS
                q, dj = (w + v) % WS, (w + v) // WS
                cls = ph * WS + q
                scl = xs14 if di else xs4
                nc.tensor.matmul_mx(
                    out=accs[dj][:, b * PIX : (b + 1) * PIX],
                    lhsT=wc[:, n * O : (n + 1) * O].bitcast(FP8X4),
                    lhsT_scale=wsc[:, n * O : (n + 1) * O],
                    rhs=xc4[:, cls, b, di * NJ : di * NJ + PIX].bitcast(FP8X4),
                    rhs_scale=scl[:, cls, b, :],
                    start=(n == taps[dj][0]),
                    stop=(n == taps[dj][-1]),
                )

        def evacuate(k):
            h, w = hw(k)
            accs = state[("acc", k)]
            if w == WS - 1:
                planes = res.tile([P, WS, B * PIX], F32)
                state[("planes", h)] = planes
            planes = state[("planes", h)]
            bcol = bias_sb[:, h * WS + w : h * WS + w + 1]
            nc.scalar.activation(
                out=planes[:, w, :], in_=accs[0][:], func=IDENT, bias=bcol, scale=1.0
            )

        def combine(k):
            h, w = hw(k)
            accs = state[("acc", k)]
            planes = state[("planes", h)]
            if w + K - 1 >= WS:
                pv = planes[:, w, :].rearrange("p (r j) -> p r j", j=NJ)
                av = accs[1][:].rearrange("p (r j) -> p r j", j=NJ)
                nc.vector.tensor_tensor(
                    out=pv[:, :, 0 : NJ - 1], in0=pv[:, :, 0 : NJ - 1], in1=av[:, :, 1:NJ], op=ADD
                )
            if w == 0:
                for b in range(B):
                    ot = res.tile([P, PIX * WS], F32, bufs=3)
                    nc.vector.tensor_copy(
                        out=ot[:].rearrange("p (x w) -> p x w", w=WS),
                        in_=planes[:, :, b * PIX : (b + 1) * PIX].rearrange("p w x -> p x w"),
                    )
                    nc.sync.dma_start(
                        out=out[b].rearrange("o (i h) z -> h o i z", h=HS)[h],
                        in_=ot[:].rearrange("p (i z) -> p i z", z=W),
                    )

        QPIX = PIX // 2

        def multiply_piece(pc):
            h, w = hw(LAST)
            b, c0 = pc // 2, (pc % 2) * QPIX
            wc, wsc = state[("wc", LAST)]
            acc = psum.tile([P, B * PIX], F32, tag=("acc0" if pc in (0, 3) else "acc1"))
            for n in range(TAPS):
                u, v = n // K, n % K
                ph, di = (h + u) % HS, (h + u) // HS
                cls = ph * WS + w + v
                scl = xs14 if di else xs4
                nc.tensor.matmul_mx(
                    out=acc[:, 0:QPIX],
                    lhsT=wc[:, n * O : (n + 1) * O].bitcast(FP8X4),
                    lhsT_scale=wsc[:, n * O : (n + 1) * O],
                    rhs=xc4[:, cls, b, di * NJ + c0 : di * NJ + c0 + QPIX].bitcast(FP8X4),
                    rhs_scale=scl[:, cls, b, c0 : c0 + QPIX],
                    start=(n == 0),
                    stop=(n == TAPS - 1),
                )
            state[("piece", pc)] = acc

        def finish_piece(pc):
            h, w = hw(LAST)
            b, c0 = pc // 2, pc * QPIX
            planes = state[("planes", h)]
            if pc % 2 == 0:
                ot = res.tile([P, PIX * WS], F32, bufs=3)
                state["ot_last"] = ot
            ot = state["ot_last"]
            o0 = (pc % 2) * QPIX * WS
            nc.scalar.activation(
                out=planes[:, w, c0 : c0 + QPIX],
                in_=state[("piece", pc)][:, 0:QPIX],
                func=IDENT,
                bias=bias_sb[:, h * WS + w : h * WS + w + 1],
                scale=1.0,
            )
            nc.vector.tensor_copy(
                out=ot[:, o0 : o0 + QPIX * WS].rearrange("p (x w) -> p x w", w=WS),
                in_=planes[:, :, c0 : c0 + QPIX].rearrange("p w x -> p x w"),
            )
            i0 = (pc % 2) * (NI // 2)
            nc.sync.dma_start(
                out=out[b].rearrange("o (i h) z -> h o i z", h=HS)[h][:, i0 : i0 + NI // 2, :],
                in_=ot[:, o0 : o0 + QPIX * WS].rearrange("p (i z) -> p i z", z=W),
            )

        ALLG = (0, 1, 2)

        load_x(0)
        load_x(1)
        load_w(0)
        load_x(2)
        sort_w(0, ALLG)
        regroup_x(0)
        load_x(3)
        load_bias()
        load_w(1)
        bias_transpose()
        regroup_x(1)
        load_x(4)
        sort_w(1, ALLG)
        transposes(0)
        regroup_x(2)
        load_x(5)
        load_w(2)
        quantise_x(0)
        bias_copy()
        regroup_x(3)
        load_x(6)
        quantise_x(1)
        sort_w(2, ALLG)
        transposes(1)
        regroup_x(4)
        load_x(7)
        load_w(3)
        quantise_x(2)
        regroup_x(5)
        load_x(8)
        quantise_x(3)
        load_w(4)
        quantise_w(0)
        multiply(0, 0)
        sort_w(3, ALLG)
        transposes(2)
        regroup_x(6)
        quantise_x(4)
        load_w(5)
        regroup_x(7)
        quantise_x(5)
        quantise_w(1)
        multiply(1, 0)
        transposes(3)
        regroup_x(8)
        quantise_x(6)
        load_w(6)
        quantise_x(7)
        quantise_w(2)

        ctx.enter_context(tc.manual_schedule(engines={mybir.EngineType.PE}))
        TCUT = 4
        pending = []
        for s in range(LAST - 1):
            a = NHEAD + s
            if a + 3 < NCLS:
                load_w(a + 3)
            for k in pending:
                evacuate(k)
            if a < NCLS:
                sort_w(a, (0,))
            if NHEAD <= a - 2 < NCLS:
                quantise_w(a - 2)
            for k in pending:
                combine(k)
            pending = []
            turn = NHEAD <= a - 1 < NCLS
            if s == 0:
                multiply(0, 1)
                multiply(1, 1)
                pending = [0, 1]
            elif s + 1 < LAST:
                pending = [s + 1]
                multiply(s + 1, 0)
                if turn:
                    transposes(a - 1, 0, TCUT)
                multiply(s + 1, 1)
            if a < NCLS:
                sort_w(a, (1, 2))
            if s == 0:
                quantise_w(NHEAD - 1)
            if turn:
                transposes(a - 1, TCUT, TAPS)

        for pc in range(3):
            multiply_piece(pc)
        evacuate(LAST - 1)
        combine(LAST - 1)
        multiply_piece(3)
        for pc in range(4):
            finish_piece(pc)
